import numpy as np
import ml_dtypes


BF16 = ml_dtypes.bfloat16


def bf(x):
    return np.asarray(x, np.float32).astype(BF16)


def f64(x):
    return np.asarray(x).astype(np.float64)


E2M1 = np.array([0.0, 0.5, 1.0, 1.5, 2.0, 3.0, 4.0, 6.0, -0.0, -0.5, -1.0, -1.5, -2.0, -3.0, -4.0, -6.0])


def pack_weight(w, fmt):
    k, n = w.shape
    w = f64(bf(w)).reshape(k // 32, 32, n)
    amax = np.abs(w).max(1)
    if fmt == "e4m3":
        byte = np.frexp(amax)[1] - 1 + 127 - 7
    else:
        mant, ex = np.frexp(amax / 6.0)
        byte = np.where(mant > 0.5, ex, ex - 1) + 127
    byte = np.clip(np.where(amax > 0, byte, 1), 1, 254)
    scaled = (w * np.exp2(127.0 - byte)[:, None, :]).reshape(k, n).astype(np.float32)
    by_word = np.ascontiguousarray(scaled.reshape(k // 512, 128, 4, n).transpose(0, 1, 3, 2))
    if fmt == "e4m3":
        words = by_word.astype(ml_dtypes.float8_e4m3fn).view(np.uint8)
    else:
        c = by_word.astype(ml_dtypes.float4_e2m1fn).view(np.uint8) & 0xF
        words = c[..., 0::2] | (c[..., 1::2] << 4)
    return np.ascontiguousarray(words), np.ascontiguousarray(byte.astype(np.uint8).reshape(k // 512, 16, n))


def unpack_weight(words, scales, fmt):
    g, p, n, _ = words.shape
    if fmt == "e4m3":
        vals = np.ascontiguousarray(words).view(ml_dtypes.float8_e4m3fn).astype(np.float64)
    else:
        nib = np.empty((g, p, n, 4), np.uint8)
        nib[..., 0::2] = words & 0xF
        nib[..., 1::2] = words >> 4
        vals = E2M1[nib]
    vals = vals * np.repeat(np.exp2(scales.astype(np.float64) - 127.0), 8, axis=1)[..., None]
    return vals.transpose(0, 1, 3, 2).reshape(g * 512, n)

def pack4(w):
    words, scales = pack_weight(w, "e2m1")
    return words.reshape(words.shape[0], 128, -1), scales


def unpack4(words, scales):
    return unpack_weight(words.reshape(words.shape[0], 128, -1, 2), scales, "e2m1")


def kspread(k):
    return np.exp2(np.repeat(np.random.randint(-6, 7, k // 32), 32).astype(np.float64))


B, T, D, DH, H, W = 1, 2048, 4096, 512, 4, 512
ROPE_BASE = 10000.0
EPS = 1.1920929e-07


def rope(u):
    freqs = ROPE_BASE ** (-2.0 * np.arange(DH // 2) / DH)
    theta = np.arange(T)[:, None] * freqs[None, :]
    cos, sin = np.cos(theta), np.sin(theta)
    u1, u2 = u[..., 0::2], u[..., 1::2]
    return np.stack([u1 * cos - u2 * sin, u1 * sin + u2 * cos], axis=-1).reshape(u.shape)


def rmsnorm(u, w):
    return u * (1.0 / np.sqrt(np.mean(u * u, axis=-1, keepdims=True) + EPS)) * w


def setup_inputs():
    s = kspread(D)
    x = np.random.standard_normal((B, T, D)) * s
    wq = np.random.standard_normal((H * DH, D)) / np.sqrt(D) / s
    wkv = np.random.standard_normal((2 * DH, D)) * 2.0 / np.sqrt(D) / s
    q_norm_w = bf(1.0 + 0.1 * np.random.standard_normal(DH))
    k_norm_w = bf(1.0 + 0.1 * np.random.standard_normal(DH))
    x_words, x_scales = pack4(np.ascontiguousarray(x.reshape(B * T, D).T))
    wq_words, wq_scales = pack4(np.ascontiguousarray(wq.T))
    wkv_words, wkv_scales = pack4(np.ascontiguousarray(wkv.T))
    return {"x_words": x_words, "x_scales": x_scales,
            "wq_words": wq_words, "wq_scales": wq_scales,
            "wkv_words": wkv_words, "wkv_scales": wkv_scales,
            "q_norm_w": q_norm_w,
            "k_norm_w": k_norm_w}


def reference(x_words, x_scales, wq_words, wq_scales, wkv_words, wkv_scales, q_norm_w, k_norm_w):
    xq = unpack4(x_words, x_scales).T.reshape(B, T, D)
    q = xq @ unpack4(wq_words, wq_scales)
    kv = xq @ unpack4(wkv_words, wkv_scales)
    k, v = kv[..., :DH], kv[..., DH:]
    q = q.reshape(B, T, H, DH).transpose(0, 2, 1, 3)
    q_rot = rmsnorm(rope(q), f64(q_norm_w))
    k_rot = rmsnorm(rope(k), f64(k_norm_w))
    return q_rot, k_rot, v

@@ -1,0 +1,311 @@
+from contextlib import ExitStack
+
+import concourse.mybir as mybir
+
+FLOPS = 2 * 2048 * 4096 * 3072
+
+F32 = mybir.dt.float32
+BF16 = mybir.dt.bfloat16
+I32 = mybir.dt.int32
+U8 = mybir.dt.uint8
+FP4X4 = mybir.dt.float4_e2m1fn_x4
+ALU = mybir.AluOpType
+ACT = mybir.ActivationFunctionType
+
+P = 128
+G = 8
+DH = 512
+PAIRS = DH // 2
+MT = 16
+HALF = 8
+SWEEP = 7
+PI = 3.141592653589793
+EPS = 1.1920929e-07
+ROPE_STEP = 10000.0 ** (-1.0 / PAIRS)
+
+N_WARM = 56
+BLK_K = 0
+BLK_V = 5
+
+
+def tile_attention_pa_kernel(
+    tc, x_words, x_scales, wq_words, wq_scales, wkv_words, wkv_scales, q_norm_w, k_norm_w, out_0, out_1, out_2
+):
+    nc = tc.nc
+    with ExitStack() as ctx:
+        keep = ctx.enter_context(tc.tile_pool(name="keep", bufs=1))
+        tabs = ctx.enter_context(tc.tile_pool(name="tabs", bufs=2))
+        tmp = ctx.enter_context(tc.tile_pool(name="tmp", bufs=2))
+        work = ctx.enter_context(tc.tile_pool(name="work", bufs=3))
+        outs = ctx.enter_context(tc.tile_pool(name="outs", bufs=8))
+        small = ctx.enter_context(tc.tile_pool(name="small", bufs=4))
+        gpsum = ctx.enter_context(tc.psum_pool(name="gpsum", bufs=1))
+        psum = ctx.enter_context(tc.psum_pool(name="psum", bufs=7))
+        ctx.enter_context(tc.manual_schedule())
+
+        def shifted(name, width, off):
+            whole_tile = keep.tile([P, G * width + 256], U8, name=name, align_bytes=256)
+            return whole_tile[:, off : off + G * width].rearrange("p (g b) -> p g b", g=G)
+
+        x_c = []
+        x_s = []
+        for hx in range(2):
+            x_c.append(shifted("x_c%d" % hx, 2 * P * HALF, 0))
+            x_s.append(shifted("x_s%d" % hx, P * HALF, 64))
+        w_c = []
+        w_s = []
+        for blk in range(6):
+            w_c.append(shifted("w_c%d" % blk, 2 * DH, 128))
+            w_s.append(shifted("w_s%d" % blk, DH, 192))
+
+        x_c_src = [x_words[:, :, 0:2048], x_words[:, :, 2048:4096]]
+        x_s_src = [x_scales[:, :, 0:1024], x_scales[:, :, 1024:2048]]
+        w_c_src = [wkv_words[:, :, 0:1024]]
+        w_s_src = [wkv_scales[:, :, 0:512]]
+        for h in range(4):
+            w_c_src.append(wq_words[:, :, 1024 * h : 1024 * (h + 1)])
+            w_s_src.append(wq_scales[:, :, 512 * h : 512 * (h + 1)])
+        w_c_src.append(wkv_words[:, :, 1024:2048])
+        w_s_src.append(wkv_scales[:, :, 512:1024])
+
+        def load_codes(dst, src, g0, g1):
+            nc.sync.dma_start(
+                out=dst[:, g0:g1, :].bitcast(I32),
+                in_=src[g0:g1, :, :].rearrange("g p b -> p g b").bitcast(I32),
+            )
+
+        def load_scales(dst, src, g0, g1):
+            for r in range(4):
+                nc.sync.dma_start(
+                    out=dst[r : P : 32, g0:g1, :].bitcast(I32),
+                    in_=src[g0:g1, r : 16 : 4, :].rearrange("g q n -> q g n").bitcast(I32),
+                )
+
+        def zero_vector(plane, g0, g1):
+            nc.vector.memset(plane[:, g0:g1, :].bitcast(I32), 0)
+
+        def zero_gpsimd(plane):
+            nc.gpsimd.memset(plane[:].bitcast(F32), 0.0)
+
+        zero_vector(x_s[0], 0, 1)
+        zero_vector(w_s[BLK_V], 0, G)
+        zero_vector(x_s[0], 1, G)
+        gz = keep.tile([P, 2 * DH], BF16, name="gz")
+        nc.vector.memset(gz[:, 0:2], 0.0)
+
+        ones = keep.tile([P, P], BF16, name="ones")
+        nc.gpsimd.memset(ones[:], 1.0)
+        zero1 = keep.tile([P, 1], F32, name="zero1")
+        nc.gpsimd.memset(zero1[:], 0.0)
+        pos_i = keep.tile([P, MT], I32, name="pos_i")
+        nc.gpsimd.iota(pos_i[:], pattern=[[P, MT]], base=0, channel_multiplier=1)
+        nc.gpsimd.memset(gz[:], 0.0)
+        for blk in range(5):
+            zero_gpsimd(w_s[blk])
+
+        gains = gpsum.tile([P, 2 * DH], BF16, name="gains")
+        for rep_i in range(N_WARM):
+            nc.tensor.matmul(out=gains[:, 0:P], lhsT=ones[:], rhs=ones[:], start=True, stop=True)
+        nc.gpsimd.dma_start(out=gz[0:1, 0:DH], in_=q_norm_w.rearrange("(o n) -> o n", o=1))
+        nc.gpsimd.dma_start(out=gz[0:1, DH : 2 * DH], in_=k_norm_w.rearrange("(o n) -> o n", o=1))
+        zero_gpsimd(x_s[1])
+
+        load_codes(x_c[0], x_c_src[0], 0, 1)
+        load_codes(w_c[BLK_V], w_c_src[BLK_V], 0, 1)
+        load_scales(x_s[0], x_s_src[0], 0, 1)
+        load_scales(w_s[BLK_V], w_s_src[BLK_V], 0, G)
+        load_codes(x_c[0], x_c_src[0], 1, 2)
+        load_codes(w_c[BLK_V], w_c_src[BLK_V], 1, G)
+        load_scales(x_s[0], x_s_src[0], 1, G)
+        load_codes(x_c[0], x_c_src[0], 2, 4)
+        load_codes(x_c[0], x_c_src[0], 4, G)
+        for blk in range(5):
+            load_codes(w_c[blk], w_c_src[blk], 0, G)
+            load_scales(w_s[blk], w_s_src[blk], 0, G)
+
+        warm = small.tile([P, 1], F32, name="warm")
+        nc.scalar.activation(out=warm[:], in_=zero1[:], func=ACT.Sin)
+
+        one1 = keep.tile([P, 1], F32, name="one1")
+        nc.vector.memset(one1[:], 1.0)
+        frq = keep.tile([P, PAIRS], F32, name="frq")
+        nc.vector.tensor_scalar(out=frq[:, 0:1], in0=one1[:], scalar1=1.0 / (2.0 * PI), scalar2=None, op0=ALU.mult)
+        width = 1
+        while width < PAIRS:
+            nc.vector.tensor_scalar(
+                out=frq[:, width : 2 * width],
+                in0=frq[:, 0:width],
+                scalar1=ROPE_STEP**width,
+                scalar2=None,
+                op0=ALU.mult,
+            )
+            width = 2 * width
+        pos = keep.tile([P, MT], F32, name="pos")
+        nc.vector.tensor_copy(out=pos[:], in_=pos_i[:])
+
+        cos_raw = keep.tile([P, MT, PAIRS], F32, name="cos_raw")
+        sin_raw = keep.tile([P, MT, 2, PAIRS], F32, name="sin_raw")
+        for m in range(MT):
+            whole = tmp.tile([P, PAIRS], I32, name="whole")
+            nc.vector.tensor_scalar(out=whole[:], in0=frq[:], scalar1=pos[:, m : m + 1], scalar2=None, op0=ALU.mult)
+            nfr = tmp.tile([P, PAIRS], F32, name="nfr", bufs=8)
+            nc.vector.scalar_tensor_tensor(
+                out=nfr[:], in0=frq[:], scalar=pos[:, m : m + 1], in1=whole[:], op0=ALU.mult, op1=ALU.subtract
+            )
+            nc.scalar.activation(out=sin_raw[:, m, 0, :], in_=nfr[:], func=ACT.Sin, scale=-2.0 * PI)
+            nc.scalar.activation(out=sin_raw[:, m, 1, :], in_=nfr[:], func=ACT.Sin, scale=2.0 * PI)
+            mag = tmp.tile([P, PAIRS], F32, name="mag")
+            nc.scalar.activation(out=mag[:], in_=nfr[:], func=ACT.Abs)
+            nc.scalar.activation(out=cos_raw[:, m, :], in_=mag[:], func=ACT.Sin, scale=-2.0 * PI, bias=PI / 2.0)
+
+
+        def pairs(ap):
+            return ap.rearrange("p (i t) -> p i t", t=2)
+
+        def cos_view(m):
+            return cos_raw[:, m, :].unsqueeze(2).to_broadcast([P, PAIRS, 2])
+
+        def sin_view(m):
+            return sin_raw[:, m, :, :].rearrange("p t i -> p i t")
+
+        def fold(m):
+            gain = pairs(gains[:, 0:DH])
+            ctab = tabs.tile([P, DH], F32, name="ctab")
+            nc.vector.tensor_tensor(
+                out=pairs(ctab[:]),
+                in0=gain,
+                in1=cos_view(m),
+                op=ALU.mult,
+            )
+            stab = tabs.tile([P, DH], F32, name="stab")
+            nc.vector.tensor_tensor(
+                out=pairs(stab[:]),
+                in0=gain,
+                in1=sin_view(m),
+                op=ALU.mult,
+            )
+            return (pairs(ctab[:]), pairs(stab[:]))
+
+        def mx_pass(acc, m, blk, g, c0, cols):
+            xc = x_c[m // HALF]
+            xs = x_s[m // HALF]
+            mm = m % HALF
+            nc.tensor.matmul_mx(
+                out=acc,
+                lhsT=xc[:, g, 2 * P * mm : 2 * P * (mm + 1)].bitcast(FP4X4),
+                lhsT_scale=xs[:, g, P * mm : P * (mm + 1)],
+                rhs=w_c[blk][:, g, 2 * c0 : 2 * (c0 + cols)].bitcast(FP4X4),
+                rhs_scale=w_s[blk][:, g, c0 : c0 + cols],
+                start=(g == 0),
+                stop=(g == G - 1),
+            )
+
+        def rows(m):
+            return slice(P * m, P * (m + 1))
+
+        def v_out(acc, m, c0, cols, on_vector):
+            res = outs.tile([P, DH], F32, name="res")
+            if on_vector:
+                nc.vector.tensor_copy(out=res[:, 0:cols], in_=acc)
+            else:
+                nc.scalar.copy(out=res[:, 0:cols], in_=acc)
+            nc.sync.dma_start(out=out_2[0, rows(m), c0 : c0 + cols], in_=res[:, 0:cols])
+
+        def rope_norm(acc):
+            junk = work.tile([P, DH], BF16, name="junk")
+            ssq = small.tile([P, 1], F32, name="ssq")
+            nc.scalar.activation(out=junk[:], in_=acc[:], func=ACT.Square, accum_out=ssq[:])
+            std = small.tile([P, 1], F32, name="std")
+            nc.scalar.activation(out=std[:], in_=ssq[:], func=ACT.Sqrt, scale=1.0 / DH, bias=EPS)
+            rstd = small.tile([P, 1], F32, name="rstd")
+            nc.vector.reciprocal(out=rstd[:], in_=std[:])
+            return rstd
+
+        def rope_out(acc, m, blk, rstd):
+            if blk == BLK_K:
+                ctab = cos_view(m)
+                stab = sin_view(m)
+            else:
+                ctab, stab = made[m]
+            res = outs.tile([P, DH], F32, name="res")
+            nc.vector.scalar_tensor_tensor(
+                out=pairs(res[:]), in0=pairs(acc[:]), scalar=rstd[:, 0:1], in1=ctab, op0=ALU.mult, op1=ALU.mult
+            )
+            cross = work.tile([P, DH], F32, name="cross")
+            nc.vector.scalar_tensor_tensor(
+                out=pairs(cross[:]),
+                in0=pairs(acc[:])[:, :, ::-1],
+                scalar=rstd[:, 0:1],
+                in1=stab,
+                op0=ALU.mult,
+                op1=ALU.mult,
+            )
+            nc.gpsimd.tensor_tensor(out=res[:], in0=res[:], in1=cross[:], op=ALU.add)
+            if blk == BLK_K:
+                nc.gpsimd.tensor_tensor(out=res[:], in0=res[:], in1=gain_k[:], op=ALU.mult)
+                dst = out_1[0, rows(m), :]
+            else:
+                dst = out_0[0, blk - 1, rows(m), :]
+            nc.sync.dma_start(out=dst, in_=res[:])
+
+        first = []
+        for m in range(SWEEP):
+            first.append(psum.tile([P, DH], F32, name="acc"))
+        for g in range(G):
+            for m in range(SWEEP):
+                mx_pass(first[m][:], m, BLK_V, g, 0, DH)
+            if g == G - 1:
+                nc.tensor.matmul(out=gains[:, 0:DH], lhsT=ones[:], rhs=gz[:, 0:DH], start=True, stop=True)
+                nc.tensor.matmul(
+                    out=gains[:, DH : 2 * DH], lhsT=ones[:], rhs=gz[:, DH : 2 * DH], start=True, stop=True
+                )
+        for m in range(SWEEP):
+            v_out(first[m][:], m, 0, DH, True)
+        gain_k = keep.tile([P, DH], F32, name="gain_k")
+        nc.scalar.copy(out=gain_k[:], in_=gains[:, DH : 2 * DH])
+        seq = []
+        for m in range(SWEEP):
+            seq.append((m, BLK_K))
+        for m in range(SWEEP):
+            for blk in range(1, 5):
+                seq.append((m, blk))
+        for m in range(SWEEP, MT):
+            for blk in range(5):
+                seq.append((m, blk))
+            if m < MT - 3:
+                seq.append((m, BLK_V))
+        for m in range(MT - 3, MT - 1):
+            seq.append((m, BLK_V))
+
+        made = {}
+
+        def ensure(j):
+            if j < len(seq) and seq[j][1] != BLK_V and seq[j][1] != BLK_K:
+                if seq[j][0] not in made:
+                    made[seq[j][0]] = fold(seq[j][0])
+
+        waiting = []
+        for j, (m, blk) in enumerate(seq):
+            acc = psum.tile([P, DH], F32, name="acc")
+            for g in range(G):
+                mx_pass(acc[:], m, blk, g, 0, DH)
+            if blk != BLK_V:
+                rstd = rope_norm(acc)
+            for held in waiting:
+                rope_out(*held)
+            waiting.clear()
+            if blk == BLK_V:
+                v_out(acc[:], m, 0, DH, False)
+            else:
+                waiting.append((acc, m, blk, rstd))
+            ensure(j + 1)
+            if j == 9:
+                load_codes(x_c[1], x_c_src[1], 0, 4)
+                load_codes(x_c[1], x_c_src[1], 4, G)
+                load_scales(x_s[1], x_s_src[1], 0, G)
+
+        for part in range(2):
+            acc = psum.tile([P, DH // 2], F32, name="acc")
+            for g in range(G):
+                mx_pass(acc[:], MT - 1, BLK_V, g, part * (DH // 2), DH // 2)
+            v_out(acc[:], MT - 1, part * (DH // 2), DH // 2, part == 1)

@@ -44,19 +44,19 @@ def tile_attention_pa_kernel(
         ctx.enter_context(tc.manual_schedule())
 
         def shifted(name, width, off):
-            whole_tile = keep.tile([P, G * width + 256], U8, name=name, align_bytes=256)
+            whole_tile = keep.tile([P, G * width], U8, name=name, align_bytes=256)
             return whole_tile[:, off : off + G * width].rearrange("p (g b) -> p g b", g=G)
 
         x_c = []
         x_s = []
         for hx in range(2):
             x_c.append(shifted("x_c%d" % hx, 2 * P * HALF, 0))
-            x_s.append(shifted("x_s%d" % hx, P * HALF, 64))
+            x_s.append(shifted("x_s%d" % hx, P * HALF, 0))
         w_c = []
         w_s = []
         for blk in range(6):
-            w_c.append(shifted("w_c%d" % blk, 2 * DH, 128))
-            w_s.append(shifted("w_s%d" % blk, DH, 192))
+            w_c.append(shifted("w_c%d" % blk, 2 * DH, 0))
+            w_s.append(shifted("w_s%d" % blk, DH, 0))
 
         x_c_src = [x_words[:, :, 0:2048], x_words[:, :, 2048:4096]]
         x_s_src = [x_scales[:, :, 0:1024], x_scales[:, :, 1024:2048]]
@@ -100,6 +100,7 @@ def tile_attention_pa_kernel(
         pos_i = keep.tile([P, MT], I32, name="pos_i")
         nc.gpsimd.iota(pos_i[:], pattern=[[P, MT]], base=0, channel_multiplier=1)
         nc.gpsimd.memset(gz[:], 0.0)
+        zero_gpsimd(x_s[1])
         for blk in range(5):
             zero_gpsimd(w_s[blk])
 
@@ -108,7 +109,6 @@ def tile_attention_pa_kernel(
             nc.tensor.matmul(out=gains[:, 0:P], lhsT=ones[:], rhs=ones[:], start=True, stop=True)
         nc.gpsimd.dma_start(out=gz[0:1, 0:DH], in_=q_norm_w.rearrange("(o n) -> o n", o=1))
         nc.gpsimd.dma_start(out=gz[0:1, DH : 2 * DH], in_=k_norm_w.rearrange("(o n) -> o n", o=1))
-        zero_gpsimd(x_s[1])
 
         load_codes(x_c[0], x_c_src[0], 0, 1)
         load_codes(w_c[BLK_V], w_c_src[BLK_V], 0, 1)
@@ -119,6 +119,9 @@ def tile_attention_pa_kernel(
         load_scales(x_s[0], x_s_src[0], 1, G)
         load_codes(x_c[0], x_c_src[0], 2, 4)
         load_codes(x_c[0], x_c_src[0], 4, G)
+        load_codes(x_c[1], x_c_src[1], 0, 4)
+        load_codes(x_c[1], x_c_src[1], 4, G)
+        load_scales(x_s[1], x_s_src[1], 0, G)
         for blk in range(5):
             load_codes(w_c[blk], w_c_src[blk], 0, G)
             load_scales(w_s[blk], w_s_src[blk], 0, G)
@@ -203,13 +206,14 @@ def tile_attention_pa_kernel(
         def rows(m):
             return slice(P * m, P * (m + 1))
 
-        def v_out(acc, m, c0, cols, on_vector):
+        def v_out(acc, m, c0, cols, on_vector, early=False):
             res = outs.tile([P, DH], F32, name="res")
             if on_vector:
                 nc.vector.tensor_copy(out=res[:, 0:cols], in_=acc)
             else:
                 nc.scalar.copy(out=res[:, 0:cols], in_=acc)
-            nc.sync.dma_start(out=out_2[0, rows(m), c0 : c0 + cols], in_=res[:, 0:cols])
+            queue = nc.gpsimd if early else nc.sync
+            queue.dma_start(out=out_2[0, rows(m), c0 : c0 + cols], in_=res[:, 0:cols])
 
         def rope_norm(acc):
             junk = work.tile([P, DH], BF16, name="junk")
@@ -260,10 +264,13 @@ def tile_attention_pa_kernel(
                     out=gains[:, DH : 2 * DH], lhsT=ones[:], rhs=gz[:, DH : 2 * DH], start=True, stop=True
                 )
         for m in range(SWEEP):
-            v_out(first[m][:], m, 0, DH, True)
+            v_out(first[m][:], m, 0, DH, True, early=True)
         gain_k = keep.tile([P, DH], F32, name="gain_k")
         nc.scalar.copy(out=gain_k[:], in_=gains[:, DH : 2 * DH])
         seq = []
+        for m in range(SWEEP, MT - 3):
+            seq.append((m, BLK_V))
+        n_early = len(seq)
         for m in range(SWEEP):
             seq.append((m, BLK_K))
         for m in range(SWEEP):
@@ -272,8 +279,6 @@ def tile_attention_pa_kernel(
         for m in range(SWEEP, MT):
             for blk in range(5):
                 seq.append((m, blk))
-            if m < MT - 3:
-                seq.append((m, BLK_V))
         for m in range(MT - 3, MT - 1):
             seq.append((m, BLK_V))
 
@@ -295,14 +300,10 @@ def tile_attention_pa_kernel(
                 rope_out(*held)
             waiting.clear()
             if blk == BLK_V:
-                v_out(acc[:], m, 0, DH, False)
+                v_out(acc[:], m, 0, DH, j < n_early, early=(j < n_early))
             else:
                 waiting.append((acc, m, blk, rstd))
             ensure(j + 1)
-            if j == 9:
-                load_codes(x_c[1], x_c_src[1], 0, 4)
-                load_codes(x_c[1], x_c_src[1], 4, G)
-                load_scales(x_s[1], x_s_src[1], 0, G)
 
         for part in range(2):
             acc = psum.tile([P, DH // 2], F32, name="acc")

@@ -84,14 +84,11 @@ def tile_attention_pa_kernel(
         def zero_vector(plane, g0, g1):
             nc.vector.memset(plane[:, g0:g1, :].bitcast(I32), 0)
 
-        def zero_gpsimd(plane):
-            nc.gpsimd.memset(plane[:].bitcast(F32), 0.0)
-
         zero_vector(x_s[0], 0, 1)
         zero_vector(w_s[BLK_V], 0, G)
         zero_vector(x_s[0], 1, G)
         gz = keep.tile([P, 2 * DH], BF16, name="gz")
-        nc.vector.memset(gz[:, 0:2], 0.0)
+        nc.vector.memset(gz[:], 0.0)
 
         ones = keep.tile([P, P], BF16, name="ones")
         nc.gpsimd.memset(ones[:], 1.0)
@@ -99,10 +96,6 @@ def tile_attention_pa_kernel(
         nc.gpsimd.memset(zero1[:], 0.0)
         pos_i = keep.tile([P, MT], I32, name="pos_i")
         nc.gpsimd.iota(pos_i[:], pattern=[[P, MT]], base=0, channel_multiplier=1)
-        nc.gpsimd.memset(gz[:], 0.0)
-        zero_gpsimd(x_s[1])
-        for blk in range(5):
-            zero_gpsimd(w_s[blk])
 
         gains = gpsum.tile([P, 2 * DH], BF16, name="gains")
         for rep_i in range(N_WARM):
@@ -121,10 +114,6 @@ def tile_attention_pa_kernel(
         load_codes(x_c[0], x_c_src[0], 4, G)
         load_codes(x_c[1], x_c_src[1], 0, 4)
         load_codes(x_c[1], x_c_src[1], 4, G)
-        load_scales(x_s[1], x_s_src[1], 0, G)
-        for blk in range(5):
-            load_codes(w_c[blk], w_c_src[blk], 0, G)
-            load_scales(w_s[blk], w_s_src[blk], 0, G)
 
         warm = small.tile([P, 1], F32, name="warm")
         nc.scalar.activation(out=warm[:], in_=zero1[:], func=ACT.Sin)
@@ -148,9 +137,16 @@ def tile_attention_pa_kernel(
 
         cos_raw = keep.tile([P, MT, PAIRS], F32, name="cos_raw")
         sin_raw = keep.tile([P, MT, 2, PAIRS], F32, name="sin_raw")
-        for m in range(MT):
+        def whole_turns(m):
             whole = tmp.tile([P, PAIRS], I32, name="whole")
             nc.vector.tensor_scalar(out=whole[:], in0=frq[:], scalar1=pos[:, m : m + 1], scalar2=None, op0=ALU.mult)
+            return whole
+
+        ahead = whole_turns(0)
+        for m in range(MT):
+            whole = ahead
+            if m + 1 < MT:
+                ahead = whole_turns(m + 1)
             nfr = tmp.tile([P, PAIRS], F32, name="nfr", bufs=8)
             nc.vector.scalar_tensor_tensor(
                 out=nfr[:], in0=frq[:], scalar=pos[:, m : m + 1], in1=whole[:], op0=ALU.mult, op1=ALU.subtract
@@ -160,6 +156,14 @@ def tile_attention_pa_kernel(
             mag = tmp.tile([P, PAIRS], F32, name="mag")
             nc.scalar.activation(out=mag[:], in_=nfr[:], func=ACT.Abs)
             nc.scalar.activation(out=cos_raw[:, m, :], in_=mag[:], func=ACT.Sin, scale=-2.0 * PI, bias=PI / 2.0)
+            if m == HALF - 1:
+                zero_vector(x_s[1], 0, G)
+                load_scales(x_s[1], x_s_src[1], 0, G)
+                zero_vector(w_s[BLK_K], 0, G)
+                load_codes(w_c[BLK_K], w_c_src[BLK_K], 0, G)
+                load_scales(w_s[BLK_K], w_s_src[BLK_K], 0, G)
+                for blk in range(1, 5):
+                    load_codes(w_c[blk], w_c_src[blk], 0, G)
 
 
         def pairs(ap):
@@ -301,6 +305,9 @@ def tile_attention_pa_kernel(
             waiting.clear()
             if blk == BLK_V:
                 v_out(acc[:], m, 0, DH, j < n_early, early=(j < n_early))
+                if j < 4:
+                    zero_vector(w_s[j + 1], 0, G)
+                    load_scales(w_s[j + 1], w_s_src[j + 1], 0, G)
             else:
                 waiting.append((acc, m, blk, rstd))
             ensure(j + 1)

@@ -23,7 +23,7 @@ PI = 3.141592653589793
 EPS = 1.1920929e-07
 ROPE_STEP = 10000.0 ** (-1.0 / PAIRS)
 
-N_WARM = 56
+N_WARM = 80
 BLK_K = 0
 BLK_V = 5
 
@@ -74,8 +74,8 @@ def tile_attention_pa_kernel(
                 in_=src[g0:g1, :, :].rearrange("g p b -> p g b").bitcast(I32),
             )
 
-        def load_scales(dst, src, g0, g1):
-            for r in range(4):
+        def load_scales(dst, src, g0, g1, some=(0, 1, 2, 3)):
+            for r in some:
                 nc.sync.dma_start(
                     out=dst[r : P : 32, g0:g1, :].bitcast(I32),
                     in_=src[g0:g1, r : 16 : 4, :].rearrange("g q n -> q g n").bitcast(I32),
@@ -84,9 +84,9 @@ def tile_attention_pa_kernel(
         def zero_vector(plane, g0, g1):
             nc.vector.memset(plane[:, g0:g1, :].bitcast(I32), 0)
 
-        zero_vector(x_s[0], 0, 1)
+        nc.gpsimd.memset(x_s[0][:, 0:2, :].bitcast(F32), 0.0)
         zero_vector(w_s[BLK_V], 0, G)
-        zero_vector(x_s[0], 1, G)
+        zero_vector(x_s[0], 2, G)
         gz = keep.tile([P, 2 * DH], BF16, name="gz")
         nc.vector.memset(gz[:], 0.0)
 
@@ -103,15 +103,17 @@ def tile_attention_pa_kernel(
         nc.gpsimd.dma_start(out=gz[0:1, 0:DH], in_=q_norm_w.rearrange("(o n) -> o n", o=1))
         nc.gpsimd.dma_start(out=gz[0:1, DH : 2 * DH], in_=k_norm_w.rearrange("(o n) -> o n", o=1))
 
-        load_codes(x_c[0], x_c_src[0], 0, 1)
-        load_codes(w_c[BLK_V], w_c_src[BLK_V], 0, 1)
-        load_scales(x_s[0], x_s_src[0], 0, 1)
+        load_scales(x_s[0], x_s_src[0], 0, 2, (0, 1))
+        load_codes(x_c[0], x_c_src[0], 0, 2)
+        load_codes(w_c[BLK_V], w_c_src[BLK_V], 0, 2)
         load_scales(w_s[BLK_V], w_s_src[BLK_V], 0, G)
-        load_codes(x_c[0], x_c_src[0], 1, 2)
-        load_codes(w_c[BLK_V], w_c_src[BLK_V], 1, G)
-        load_scales(x_s[0], x_s_src[0], 1, G)
+        load_scales(x_s[0], x_s_src[0], 0, 2, (2, 3))
+        load_codes(w_c[BLK_V], w_c_src[BLK_V], 2, 4)
         load_codes(x_c[0], x_c_src[0], 2, 4)
-        load_codes(x_c[0], x_c_src[0], 4, G)
+        load_scales(x_s[0], x_s_src[0], 2, G)
+        load_codes(w_c[BLK_V], w_c_src[BLK_V], 4, G)
+        load_codes(x_c[0], x_c_src[0], 4, 6)
+        load_codes(x_c[0], x_c_src[0], 6, G)
         load_codes(x_c[1], x_c_src[1], 0, 4)
         load_codes(x_c[1], x_c_src[1], 4, G)
 

@@ -23,7 +23,7 @@ PI = 3.141592653589793
 EPS = 1.1920929e-07
 ROPE_STEP = 10000.0 ** (-1.0 / PAIRS)
 
-N_WARM = 80
+N_WARM = 75
 BLK_K = 0
 BLK_V = 5
 
@@ -81,14 +81,21 @@ def tile_attention_pa_kernel(
                     in_=src[g0:g1, r : 16 : 4, :].rearrange("g q n -> q g n").bitcast(I32),
                 )
 
+        def load_first_plane(some):
+            half_rows = x_scales.rearrange("g q (h c) -> (g q h) c", h=2)
+            for r in some:
+                nc.sync.dma_start(
+                    out=x_s[0][r : P : 4, 0:2, :].bitcast(I32),
+                    in_=half_rows[2 * r : 2 * r + 64, :].rearrange("(g a) c -> a g c", a=32).bitcast(I32),
+                )
+
         def zero_vector(plane, g0, g1):
             nc.vector.memset(plane[:, g0:g1, :].bitcast(I32), 0)
 
-        nc.gpsimd.memset(x_s[0][:, 0:2, :].bitcast(F32), 0.0)
-        zero_vector(w_s[BLK_V], 0, G)
-        zero_vector(x_s[0], 2, G)
         gz = keep.tile([P, 2 * DH], BF16, name="gz")
         nc.vector.memset(gz[:], 0.0)
+        zero_vector(w_s[BLK_V], 0, G)
+        zero_vector(x_s[0], 2, G)
 
         ones = keep.tile([P, P], BF16, name="ones")
         nc.gpsimd.memset(ones[:], 1.0)
@@ -102,12 +109,14 @@ def tile_attention_pa_kernel(
             nc.tensor.matmul(out=gains[:, 0:P], lhsT=ones[:], rhs=ones[:], start=True, stop=True)
         nc.gpsimd.dma_start(out=gz[0:1, 0:DH], in_=q_norm_w.rearrange("(o n) -> o n", o=1))
         nc.gpsimd.dma_start(out=gz[0:1, DH : 2 * DH], in_=k_norm_w.rearrange("(o n) -> o n", o=1))
+        nc.tensor.matmul(out=gains[:, 0:DH], lhsT=ones[:], rhs=gz[:, 0:DH], start=True, stop=True)
+        nc.tensor.matmul(out=gains[:, DH : 2 * DH], lhsT=ones[:], rhs=gz[:, DH : 2 * DH], start=True, stop=True)
 
-        load_scales(x_s[0], x_s_src[0], 0, 2, (0, 1))
+        load_first_plane((0, 1))
         load_codes(x_c[0], x_c_src[0], 0, 2)
         load_codes(w_c[BLK_V], w_c_src[BLK_V], 0, 2)
         load_scales(w_s[BLK_V], w_s_src[BLK_V], 0, G)
-        load_scales(x_s[0], x_s_src[0], 0, 2, (2, 3))
+        load_first_plane((2, 3))
         load_codes(w_c[BLK_V], w_c_src[BLK_V], 2, 4)
         load_codes(x_c[0], x_c_src[0], 2, 4)
         load_scales(x_s[0], x_s_src[0], 2, G)
@@ -264,11 +273,6 @@ def tile_attention_pa_kernel(
         for g in range(G):
             for m in range(SWEEP):
                 mx_pass(first[m][:], m, BLK_V, g, 0, DH)
-            if g == G - 1:
-                nc.tensor.matmul(out=gains[:, 0:DH], lhsT=ones[:], rhs=gz[:, 0:DH], start=True, stop=True)
-                nc.tensor.matmul(
-                    out=gains[:, DH : 2 * DH], lhsT=ones[:], rhs=gz[:, DH : 2 * DH], start=True, stop=True
-                )
         for m in range(SWEEP):
             v_out(first[m][:], m, 0, DH, True, early=True)
         gain_k = keep.tile([P, DH], F32, name="gain_k")

@@ -23,7 +23,7 @@ PI = 3.141592653589793
 EPS = 1.1920929e-07
 ROPE_STEP = 10000.0 ** (-1.0 / PAIRS)
 
-N_WARM = 75
+N_WARM = 62
 BLK_K = 0
 BLK_V = 5
 

@@ -222,7 +222,7 @@ def tile_attention_pa_kernel(
             return slice(P * m, P * (m + 1))
 
         def v_out(acc, m, c0, cols, on_vector, early=False):
-            res = outs.tile([P, DH], F32, name="res")
+            res = outs.tile([P, DH], F32, name="res", align_bytes=256)
             if on_vector:
                 nc.vector.tensor_copy(out=res[:, 0:cols], in_=acc)
             else:
@@ -246,7 +246,7 @@ def tile_attention_pa_kernel(
                 stab = sin_view(m)
             else:
                 ctab, stab = made[m]
-            res = outs.tile([P, DH], F32, name="res")
+            res = outs.tile([P, DH], F32, name="res", align_bytes=256)
             nc.vector.scalar_tensor_tensor(
                 out=pairs(res[:]), in0=pairs(acc[:]), scalar=rstd[:, 0:1], in1=ctab, op0=ALU.mult, op1=ALU.mult
             )

from contextlib import ExitStack

import concourse.mybir as mybir

FLOPS = 2 * 2048 * 4096 * 3072

F32 = mybir.dt.float32
BF16 = mybir.dt.bfloat16
I32 = mybir.dt.int32
U8 = mybir.dt.uint8
FP4X4 = mybir.dt.float4_e2m1fn_x4
ALU = mybir.AluOpType
ACT = mybir.ActivationFunctionType

P = 128
G = 8
DH = 512
PAIRS = DH // 2
MT = 16
HALF = 8
SWEEP = 7
PI = 3.141592653589793
EPS = 1.1920929e-07
ROPE_STEP = 10000.0 ** (-1.0 / PAIRS)

N_WARM = 62
BLK_K = 0
BLK_V = 5


def tile_attention_pa_kernel(
    tc, x_words, x_scales, wq_words, wq_scales, wkv_words, wkv_scales, q_norm_w, k_norm_w, out_0, out_1, out_2
):
    nc = tc.nc
    with ExitStack() as ctx:
        keep = ctx.enter_context(tc.tile_pool(name="keep", bufs=1))
        tabs = ctx.enter_context(tc.tile_pool(name="tabs", bufs=2))
        tmp = ctx.enter_context(tc.tile_pool(name="tmp", bufs=2))
        work = ctx.enter_context(tc.tile_pool(name="work", bufs=3))
        outs = ctx.enter_context(tc.tile_pool(name="outs", bufs=8))
        small = ctx.enter_context(tc.tile_pool(name="small", bufs=4))
        gpsum = ctx.enter_context(tc.psum_pool(name="gpsum", bufs=1))
        psum = ctx.enter_context(tc.psum_pool(name="psum", bufs=7))
        ctx.enter_context(tc.manual_schedule())

        def shifted(name, width, off):
            whole_tile = keep.tile([P, G * width], U8, name=name, align_bytes=256)
            return whole_tile[:, off : off + G * width].rearrange("p (g b) -> p g b", g=G)

        x_c = []
        x_s = []
        for hx in range(2):
            x_c.append(shifted("x_c%d" % hx, 2 * P * HALF, 0))
            x_s.append(shifted("x_s%d" % hx, P * HALF, 0))
        w_c = []
        w_s = []
        for blk in range(6):
            w_c.append(shifted("w_c%d" % blk, 2 * DH, 0))
            w_s.append(shifted("w_s%d" % blk, DH, 0))

        x_c_src = [x_words[:, :, 0:2048], x_words[:, :, 2048:4096]]
        x_s_src = [x_scales[:, :, 0:1024], x_scales[:, :, 1024:2048]]
        w_c_src = [wkv_words[:, :, 0:1024]]
        w_s_src = [wkv_scales[:, :, 0:512]]
        for h in range(4):
            w_c_src.append(wq_words[:, :, 1024 * h : 1024 * (h + 1)])
            w_s_src.append(wq_scales[:, :, 512 * h : 512 * (h + 1)])
        w_c_src.append(wkv_words[:, :, 1024:2048])
        w_s_src.append(wkv_scales[:, :, 512:1024])

        def load_codes(dst, src, g0, g1):
            nc.sync.dma_start(
                out=dst[:, g0:g1, :].bitcast(I32),
                in_=src[g0:g1, :, :].rearrange("g p b -> p g b").bitcast(I32),
            )

        def load_scales(dst, src, g0, g1, some=(0, 1, 2, 3)):
            for r in some:
                nc.sync.dma_start(
                    out=dst[r : P : 32, g0:g1, :].bitcast(I32),
                    in_=src[g0:g1, r : 16 : 4, :].rearrange("g q n -> q g n").bitcast(I32),
                )

        def load_first_plane(some):
            half_rows = x_scales.rearrange("g q (h c) -> (g q h) c", h=2)
            for r in some:
                nc.sync.dma_start(
                    out=x_s[0][r : P : 4, 0:2, :].bitcast(I32),
                    in_=half_rows[2 * r : 2 * r + 64, :].rearrange("(g a) c -> a g c", a=32).bitcast(I32),
                )

        def zero_vector(plane, g0, g1):
            nc.vector.memset(plane[:, g0:g1, :].bitcast(I32), 0)

        gz = keep.tile([P, 2 * DH], BF16, name="gz")
        nc.vector.memset(gz[:], 0.0)
        zero_vector(w_s[BLK_V], 0, G)
        zero_vector(x_s[0], 2, G)

        ones = keep.tile([P, P], BF16, name="ones")
        nc.gpsimd.memset(ones[:], 1.0)
        zero1 = keep.tile([P, 1], F32, name="zero1")
        nc.gpsimd.memset(zero1[:], 0.0)
        pos_i = keep.tile([P, MT], I32, name="pos_i")
        nc.gpsimd.iota(pos_i[:], pattern=[[P, MT]], base=0, channel_multiplier=1)

        gains = gpsum.tile([P, 2 * DH], BF16, name="gains")
        for rep_i in range(N_WARM):
            nc.tensor.matmul(out=gains[:, 0:P], lhsT=ones[:], rhs=ones[:], start=True, stop=True)
        nc.gpsimd.dma_start(out=gz[0:1, 0:DH], in_=q_norm_w.rearrange("(o n) -> o n", o=1))
        nc.gpsimd.dma_start(out=gz[0:1, DH : 2 * DH], in_=k_norm_w.rearrange("(o n) -> o n", o=1))
        nc.tensor.matmul(out=gains[:, 0:DH], lhsT=ones[:], rhs=gz[:, 0:DH], start=True, stop=True)
        nc.tensor.matmul(out=gains[:, DH : 2 * DH], lhsT=ones[:], rhs=gz[:, DH : 2 * DH], start=True, stop=True)

        load_first_plane((0, 1))
        load_codes(x_c[0], x_c_src[0], 0, 2)
        load_codes(w_c[BLK_V], w_c_src[BLK_V], 0, 2)
        load_scales(w_s[BLK_V], w_s_src[BLK_V], 0, G)
        load_first_plane((2, 3))
        load_codes(w_c[BLK_V], w_c_src[BLK_V], 2, 4)
        load_codes(x_c[0], x_c_src[0], 2, 4)
        load_scales(x_s[0], x_s_src[0], 2, G)
        load_codes(w_c[BLK_V], w_c_src[BLK_V], 4, G)
        load_codes(x_c[0], x_c_src[0], 4, 6)
        load_codes(x_c[0], x_c_src[0], 6, G)
        load_codes(x_c[1], x_c_src[1], 0, 4)
        load_codes(x_c[1], x_c_src[1], 4, G)

        warm = small.tile([P, 1], F32, name="warm")
        nc.scalar.activation(out=warm[:], in_=zero1[:], func=ACT.Sin)

        one1 = keep.tile([P, 1], F32, name="one1")
        nc.vector.memset(one1[:], 1.0)
        frq = keep.tile([P, PAIRS], F32, name="frq")
        nc.vector.tensor_scalar(out=frq[:, 0:1], in0=one1[:], scalar1=1.0 / (2.0 * PI), scalar2=None, op0=ALU.mult)
        width = 1
        while width < PAIRS:
            nc.vector.tensor_scalar(
                out=frq[:, width : 2 * width],
                in0=frq[:, 0:width],
                scalar1=ROPE_STEP**width,
                scalar2=None,
                op0=ALU.mult,
            )
            width = 2 * width
        pos = keep.tile([P, MT], F32, name="pos")
        nc.vector.tensor_copy(out=pos[:], in_=pos_i[:])

        cos_raw = keep.tile([P, MT, PAIRS], F32, name="cos_raw")
        sin_raw = keep.tile([P, MT, 2, PAIRS], F32, name="sin_raw")
        def whole_turns(m):
            whole = tmp.tile([P, PAIRS], I32, name="whole")
            nc.vector.tensor_scalar(out=whole[:], in0=frq[:], scalar1=pos[:, m : m + 1], scalar2=None, op0=ALU.mult)
            return whole

        ahead = whole_turns(0)
        for m in range(MT):
            whole = ahead
            if m + 1 < MT:
                ahead = whole_turns(m + 1)
            nfr = tmp.tile([P, PAIRS], F32, name="nfr", bufs=8)
            nc.vector.scalar_tensor_tensor(
                out=nfr[:], in0=frq[:], scalar=pos[:, m : m + 1], in1=whole[:], op0=ALU.mult, op1=ALU.subtract
            )
            nc.scalar.activation(out=sin_raw[:, m, 0, :], in_=nfr[:], func=ACT.Sin, scale=-2.0 * PI)
            nc.scalar.activation(out=sin_raw[:, m, 1, :], in_=nfr[:], func=ACT.Sin, scale=2.0 * PI)
            mag = tmp.tile([P, PAIRS], F32, name="mag")
            nc.scalar.activation(out=mag[:], in_=nfr[:], func=ACT.Abs)
            nc.scalar.activation(out=cos_raw[:, m, :], in_=mag[:], func=ACT.Sin, scale=-2.0 * PI, bias=PI / 2.0)
            if m == HALF - 1:
                zero_vector(x_s[1], 0, G)
                load_scales(x_s[1], x_s_src[1], 0, G)
                zero_vector(w_s[BLK_K], 0, G)
                load_codes(w_c[BLK_K], w_c_src[BLK_K], 0, G)
                load_scales(w_s[BLK_K], w_s_src[BLK_K], 0, G)
                for blk in range(1, 5):
                    load_codes(w_c[blk], w_c_src[blk], 0, G)


        def pairs(ap):
            return ap.rearrange("p (i t) -> p i t", t=2)

        def cos_view(m):
            return cos_raw[:, m, :].unsqueeze(2).to_broadcast([P, PAIRS, 2])

        def sin_view(m):
            return sin_raw[:, m, :, :].rearrange("p t i -> p i t")

        def fold(m):
            gain = pairs(gains[:, 0:DH])
            ctab = tabs.tile([P, DH], F32, name="ctab")
            nc.vector.tensor_tensor(
                out=pairs(ctab[:]),
                in0=gain,
                in1=cos_view(m),
                op=ALU.mult,
            )
            stab = tabs.tile([P, DH], F32, name="stab")
            nc.vector.tensor_tensor(
                out=pairs(stab[:]),
                in0=gain,
                in1=sin_view(m),
                op=ALU.mult,
            )
            return (pairs(ctab[:]), pairs(stab[:]))

        def mx_pass(acc, m, blk, g, c0, cols):
            xc = x_c[m // HALF]
            xs = x_s[m // HALF]
            mm = m % HALF
            nc.tensor.matmul_mx(
                out=acc,
                lhsT=xc[:, g, 2 * P * mm : 2 * P * (mm + 1)].bitcast(FP4X4),
                lhsT_scale=xs[:, g, P * mm : P * (mm + 1)],
                rhs=w_c[blk][:, g, 2 * c0 : 2 * (c0 + cols)].bitcast(FP4X4),
                rhs_scale=w_s[blk][:, g, c0 : c0 + cols],
                start=(g == 0),
                stop=(g == G - 1),
            )

        def rows(m):
            return slice(P * m, P * (m + 1))

        def v_out(acc, m, c0, cols, on_vector, early=False):
            res = outs.tile([P, DH], F32, name="res", align_bytes=256)
            if on_vector:
                nc.vector.tensor_copy(out=res[:, 0:cols], in_=acc)
            else:
                nc.scalar.copy(out=res[:, 0:cols], in_=acc)
            queue = nc.gpsimd if early else nc.sync
            queue.dma_start(out=out_2[0, rows(m), c0 : c0 + cols], in_=res[:, 0:cols])

        def rope_norm(acc):
            junk = work.tile([P, DH], BF16, name="junk")
            ssq = small.tile([P, 1], F32, name="ssq")
            nc.scalar.activation(out=junk[:], in_=acc[:], func=ACT.Square, accum_out=ssq[:])
            std = small.tile([P, 1], F32, name="std")
            nc.scalar.activation(out=std[:], in_=ssq[:], func=ACT.Sqrt, scale=1.0 / DH, bias=EPS)
            rstd = small.tile([P, 1], F32, name="rstd")
            nc.vector.reciprocal(out=rstd[:], in_=std[:])
            return rstd

        def rope_out(acc, m, blk, rstd):
            if blk == BLK_K:
                ctab = cos_view(m)
                stab = sin_view(m)
            else:
                ctab, stab = made[m]
            res = outs.tile([P, DH], F32, name="res", align_bytes=256)
            nc.vector.scalar_tensor_tensor(
                out=pairs(res[:]), in0=pairs(acc[:]), scalar=rstd[:, 0:1], in1=ctab, op0=ALU.mult, op1=ALU.mult
            )
            cross = work.tile([P, DH], F32, name="cross")
            nc.vector.scalar_tensor_tensor(
                out=pairs(cross[:]),
                in0=pairs(acc[:])[:, :, ::-1],
                scalar=rstd[:, 0:1],
                in1=stab,
                op0=ALU.mult,
                op1=ALU.mult,
            )
            nc.gpsimd.tensor_tensor(out=res[:], in0=res[:], in1=cross[:], op=ALU.add)
            if blk == BLK_K:
                nc.gpsimd.tensor_tensor(out=res[:], in0=res[:], in1=gain_k[:], op=ALU.mult)
                dst = out_1[0, rows(m), :]
            else:
                dst = out_0[0, blk - 1, rows(m), :]
            nc.sync.dma_start(out=dst, in_=res[:])

        first = []
        for m in range(SWEEP):
            first.append(psum.tile([P, DH], F32, name="acc"))
        for g in range(G):
            for m in range(SWEEP):
                mx_pass(first[m][:], m, BLK_V, g, 0, DH)
        for m in range(SWEEP):
            v_out(first[m][:], m, 0, DH, True, early=True)
        gain_k = keep.tile([P, DH], F32, name="gain_k")
        nc.scalar.copy(out=gain_k[:], in_=gains[:, DH : 2 * DH])
        seq = []
        for m in range(SWEEP, MT - 3):
            seq.append((m, BLK_V))
        n_early = len(seq)
        for m in range(SWEEP):
            seq.append((m, BLK_K))
        for m in range(SWEEP):
            for blk in range(1, 5):
                seq.append((m, blk))
        for m in range(SWEEP, MT):
            for blk in range(5):
                seq.append((m, blk))
        for m in range(MT - 3, MT - 1):
            seq.append((m, BLK_V))

        made = {}

        def ensure(j):
            if j < len(seq) and seq[j][1] != BLK_V and seq[j][1] != BLK_K:
                if seq[j][0] not in made:
                    made[seq[j][0]] = fold(seq[j][0])

        waiting = []
        for j, (m, blk) in enumerate(seq):
            acc = psum.tile([P, DH], F32, name="acc")
            for g in range(G):
                mx_pass(acc[:], m, blk, g, 0, DH)
            if blk != BLK_V:
                rstd = rope_norm(acc)
            for held in waiting:
                rope_out(*held)
            waiting.clear()
            if blk == BLK_V:
                v_out(acc[:], m, 0, DH, j < n_early, early=(j < n_early))
                if j < 4:
                    zero_vector(w_s[j + 1], 0, G)
                    load_scales(w_s[j + 1], w_s_src[j + 1], 0, G)
            else:
                waiting.append((acc, m, blk, rstd))
            ensure(j + 1)

        for part in range(2):
            acc = psum.tile([P, DH // 2], F32, name="acc")
            for g in range(G):
                mx_pass(acc[:], MT - 1, BLK_V, g, part * (DH // 2), DH // 2)
            v_out(acc[:], MT - 1, part * (DH // 2), DH // 2, part == 1)
